import numpy as np
import ml_dtypes


def mxq(x, axis, fmt="e4m3"):
    dtype, down = {"e4m3": (ml_dtypes.float8_e4m3fn, 7), "e5m2": (ml_dtypes.float8_e5m2, 14)}[fmt]
    v = np.moveaxis(np.asarray(x, np.float32).astype(ml_dtypes.bfloat16).astype(np.float64), axis, -1)
    blocks = v.reshape(v.shape[:-1] + (-1, 32))
    amax = np.abs(blocks).max(-1, keepdims=True)
    byte = np.maximum(np.where(amax > 0, np.frexp(amax)[1] - 1 + 127, 0) - down, 1)
    scale = np.exp2(byte - 127.0)
    codes = (blocks / scale).astype(np.float32).astype(dtype).astype(np.float64)
    return np.moveaxis((codes * scale).reshape(v.shape), -1, axis)


WIDE = False


def mx_kscale(k):
    if not WIDE:
        return np.ones(k)
    levels = np.array([10, -10, 5, -5, 0])
    a = np.random.permutation(np.resize(levels, k // 512 * 4)).reshape(k // 512, 4)
    idx = np.arange(k)
    return np.exp2(a[idx // 512, idx % 128 // 32])


BF16 = ml_dtypes.bfloat16


def bf(x):
    return np.asarray(x, np.float32).astype(BF16)


def f64(x):
    return np.asarray(x).astype(np.float64)


E2M1 = np.array([0.0, 0.5, 1.0, 1.5, 2.0, 3.0, 4.0, 6.0, -0.0, -0.5, -1.0, -1.5, -2.0, -3.0, -4.0, -6.0])


def pack_weight(w, fmt):
    k, n = w.shape
    w = f64(bf(w)).reshape(k // 32, 32, n)
    amax = np.abs(w).max(1)
    if fmt == "e4m3":
        byte = np.frexp(amax)[1] - 1 + 127 - 7
    else:
        mant, ex = np.frexp(amax / 6.0)
        byte = np.where(mant > 0.5, ex, ex - 1) + 127
    byte = np.clip(np.where(amax > 0, byte, 1), 1, 254)
    scaled = (w * np.exp2(127.0 - byte)[:, None, :]).reshape(k, n).astype(np.float32)
    by_word = np.ascontiguousarray(scaled.reshape(k // 512, 128, 4, n).transpose(0, 1, 3, 2))
    if fmt == "e4m3":
        words = by_word.astype(ml_dtypes.float8_e4m3fn).view(np.uint8)
    else:
        c = by_word.astype(ml_dtypes.float4_e2m1fn).view(np.uint8) & 0xF
        words = c[..., 0::2] | (c[..., 1::2] << 4)
    return np.ascontiguousarray(words), np.ascontiguousarray(byte.astype(np.uint8).reshape(k // 512, 16, n))


def unpack_weight(words, scales, fmt):
    g, p, n, _ = words.shape
    if fmt == "e4m3":
        vals = np.ascontiguousarray(words).view(ml_dtypes.float8_e4m3fn).astype(np.float64)
    else:
        nib = np.empty((g, p, n, 4), np.uint8)
        nib[..., 0::2] = words & 0xF
        nib[..., 1::2] = words >> 4
        vals = E2M1[nib]
    vals = vals * np.repeat(np.exp2(scales.astype(np.float64) - 127.0), 8, axis=1)[..., None]
    return vals.transpose(0, 1, 3, 2).reshape(g * 512, n)


B, S, HIDDEN, N_HEADS, N_KV, HD, QB = 1, 512, 2560, 20, 5, 128, 512
QD = N_HEADS * HD
KD = N_KV * HD
FMT = "e4m3"


def apply_rope(t, cos_f, sin_f):
    n = t.shape[1]
    cos = cos_f[:n][None, :, None, :]
    sin = sin_f[:n][None, :, None, :]
    half = t.shape[-1] // 2
    t1, t2 = t[..., :half], t[..., half:]
    return t * cos + np.concatenate([-t2, t1], axis=-1) * sin


def setup_inputs():
    s = mx_kscale(HIDDEN)
    a = 1.0 / np.sqrt(HIDDEN)
    x = bf(np.random.standard_normal((B, S, HIDDEN)) * s)
    cos_f = bf(np.random.uniform(size=(S, HD)))
    sin_f = bf(np.random.uniform(size=(S, HD)))
    wq_words, wq_scales = pack_weight(np.random.standard_normal((HIDDEN, QD)) * 2.0 * a / s[:, None], FMT)
    wk_words, wk_scales = pack_weight(np.random.standard_normal((HIDDEN, KD)) * 2.0 * a / s[:, None], FMT)
    wv_words, wv_scales = pack_weight(np.random.standard_normal((HIDDEN, KD)) * a / s[:, None], FMT)
    return {"x": x,
            "cos_f": cos_f,
            "sin_f": sin_f,
            "Wq_words": wq_words, "Wq_scales": wq_scales,
            "Wk_words": wk_words, "Wk_scales": wk_scales,
            "Wv_words": wv_words, "Wv_scales": wv_scales}


def reference(x, cos_f, sin_f, Wq_words, Wq_scales, Wk_words, Wk_scales, Wv_words, Wv_scales):
    xq = mxq(f64(x), 2, "e4m3")
    q = (xq @ unpack_weight(Wq_words, Wq_scales, FMT)).reshape(B, S, N_HEADS, HD)
    k = (xq @ unpack_weight(Wk_words, Wk_scales, FMT)).reshape(B, S, N_KV, HD)
    v = (xq @ unpack_weight(Wv_words, Wv_scales, FMT)).reshape(B, S, N_KV, HD)
    return apply_rope(q, f64(cos_f), f64(sin_f)), apply_rope(k, f64(cos_f), f64(sin_f)), v

@@ -1,0 +1,205 @@
+import concourse.mybir as mybir
+from concourse.masks import make_identity
+
+F32 = mybir.dt.float32
+BF16 = mybir.dt.bfloat16
+I32 = mybir.dt.int32
+U32 = mybir.dt.uint32
+U8 = mybir.dt.uint8
+FP8X4 = mybir.dt.float8_e4m3fn_x4
+MULT = mybir.AluOpType.mult
+ADD = mybir.AluOpType.add
+
+P = 128
+PACK = 4
+K_PASS = P * PACK
+TOKENS = 512
+HIDDEN = 2560
+PASSES = HIDDEN // K_PASS
+TOKEN_TILES = TOKENS // P
+UNITS = TOKEN_TILES * PASSES
+HEAD = 128
+HALF = HEAD // 2
+Q_COLS = 20 * HEAD
+KV_COLS = 5 * HEAD
+ROPE_COLS = Q_COLS + KV_COLS
+COLS = Q_COLS + 2 * KV_COLS
+BANK = 512
+
+BLOCK_WIDTHS = [BANK // 2] + [BANK] * 7
+assert sum(BLOCK_WIDTHS) == COLS
+
+WORDS_PER_PASS = K_PASS // 2
+UNITS_PER_BANK = 2
+UNITS_PER_QUANTISE = 4
+PLANES_PER_SLOT = 4
+
+FLOPS = 2 * TOKENS * HIDDEN * COLS
+
+
+def overlap(first, width, other_first, other_width):
+    return max(first, other_first), min(first + width, other_first + other_width)
+
+
+def tile_gqattention_pa_kernel(
+    tc, x, cos_f, sin_f, Wq_words, Wq_scales, Wk_words, Wk_scales, Wv_words, Wv_scales, out_0, out_1, out_2
+):
+    nc = tc.nc
+
+    weights = []
+    for words, scales, out in ((Wq_words, Wq_scales, out_0), (Wk_words, Wk_scales, out_1), (Wv_words, Wv_scales, out_2)):
+        weights.append(
+            {
+                "first": sum(w["width"] for w in weights),
+                "width": words.shape[2],
+                "words": words.rearrange("g p n t -> p g (n t)").bitcast(I32),
+                "scales": scales.bitcast(I32),
+                "out": out[0].rearrange("(p m) h d -> m p (h d)", m=TOKEN_TILES),
+            }
+        )
+    block_firsts = [sum(BLOCK_WIDTHS[:b]) for b in range(len(BLOCK_WIDTHS))]
+
+    with tc.manual_schedule(), tc.tile_pool(name="keep", bufs=1) as keep, tc.tile_pool(
+        name="work", bufs=6
+    ) as work, tc.psum_pool(name="psum", bufs=8) as psum:
+        x_sb = keep.tile([P, TOKEN_TILES, HIDDEN], BF16)
+        grouped = keep.tile([P, UNITS, P, PACK], BF16, align_bytes=64)
+        x_codes = keep.tile([P, UNITS, P], U32, align_bytes=64)
+        x_scales = keep.tile([P, UNITS, P], U8, align_bytes=64)
+        w_codes = keep.tile([P, PASSES, COLS], U32, align_bytes=64)
+        w_scales = keep.tile([P, 2, COLS], U8, align_bytes=64)
+        identity = keep.tile([P, P], F32)
+        cos_sb = keep.tile([P, TOKEN_TILES, HEAD], BF16)
+        sin_sb = keep.tile([P, TOKEN_TILES, HEAD], BF16)
+        for_low = keep.tile([P, TOKEN_TILES, HEAD], F32)
+        for_high = keep.tile([P, TOKEN_TILES, HEAD], F32)
+
+        nc.vector.memset(w_scales[:].bitcast(I32), 0)
+        make_identity(nc, identity[:])
+
+        def load_scales(weight, slot):
+            cols = slice(weight["first"], weight["first"] + weight["width"])
+            for quadrant in range(4):
+                rows = slice(4 * quadrant, 4 * quadrant + 4)
+                if slot == 0:
+                    nc.sync.dma_start(
+                        out=w_scales[32 * quadrant : 32 * quadrant + 16, 0, cols].bitcast(I32),
+                        in_=weight["scales"][0:PLANES_PER_SLOT, rows, :],
+                    )
+                else:
+                    nc.sync.dma_start(
+                        out=w_scales[32 * quadrant : 32 * quadrant + 4, 1, cols].bitcast(I32),
+                        in_=weight["scales"][PLANES_PER_SLOT, rows, :],
+                    )
+
+        x_tiles = x[0].rearrange("(p m) k -> m p k", m=TOKEN_TILES)
+        for m in range(TOKEN_TILES):
+            nc.sync.dma_start(out=x_sb[:, m, :], in_=x_tiles[m])
+        scales_loaded = set()
+        for block_first, block_width in zip(block_firsts, BLOCK_WIDTHS):
+            touched = []
+            for weight in weights:
+                lo, hi = overlap(block_first, block_width, weight["first"], weight["width"])
+                if lo < hi:
+                    touched.append((weight, lo, hi))
+            new = [weight for weight, lo, hi in touched if weight["first"] not in scales_loaded]
+            for weight in new:
+                load_scales(weight, 0)
+            for weight, lo, hi in touched:
+                nc.sync.dma_start(
+                    out=w_codes[:, :, lo:hi].bitcast(I32),
+                    in_=weight["words"][:, :, lo - weight["first"] : hi - weight["first"]],
+                )
+            for weight in new:
+                load_scales(weight, 1)
+                scales_loaded.add(weight["first"])
+            if block_first == 0:
+                nc.sync.dma_start(out=cos_sb[:], in_=cos_f.rearrange("(p m) d -> p m d", m=TOKEN_TILES))
+                nc.sync.dma_start(out=sin_sb[:], in_=sin_f.rearrange("(p m) d -> p m d", m=TOKEN_TILES))
+
+        x_words = x_sb[:].bitcast(F32)
+        grouped_words = grouped[:].bitcast(F32)
+
+        def transpose_units(first_unit, copy):
+            bank = psum.tile([P, UNITS_PER_BANK, 2, P], F32, tag="bank")
+            for a in range(UNITS_PER_BANK):
+                m, g = divmod(first_unit + a, PASSES)
+                for u in range(2):
+                    nc.tensor.transpose(
+                        bank[:, a, u, :],
+                        x_words[:, m, WORDS_PER_PASS * g + u : WORDS_PER_PASS * (g + 1) : 2],
+                        identity[:],
+                    )
+            copy(
+                out=grouped_words[:, first_unit : first_unit + UNITS_PER_BANK, :, :],
+                in_=bank[:].rearrange("p a u t -> p a t u"),
+            )
+
+        def quantise_units(first_unit):
+            units = slice(first_unit, first_unit + UNITS_PER_QUANTISE)
+            nc.vector.quantize_mx(
+                out=x_codes[:, units, :].rearrange("p a t -> p (a t)").bitcast(FP8X4),
+                scales=x_scales[:, units, :].rearrange("p a t -> p (a t)"),
+                in_=grouped[:, units, :, :].rearrange("p a t j -> p (a t j)"),
+            )
+
+        for first_unit in range(0, UNITS, UNITS_PER_QUANTISE):
+            transpose_units(first_unit, nc.vector.tensor_copy)
+            transpose_units(first_unit + UNITS_PER_BANK, nc.scalar.copy)
+            if first_unit > 0:
+                quantise_units(first_unit - UNITS_PER_QUANTISE)
+        quantise_units(UNITS - UNITS_PER_QUANTISE)
+
+        nc.scalar.copy(out=for_low[:, :, :HALF], in_=cos_sb[:, :, :HALF])
+        nc.scalar.copy(out=for_low[:, :, HALF:], in_=sin_sb[:, :, HALF:])
+        nc.scalar.mul(out=for_high[:, :, :HALF], in_=sin_sb[:, :, :HALF], mul=-1.0)
+        nc.scalar.copy(out=for_high[:, :, HALF:], in_=cos_sb[:, :, HALF:])
+
+        for block_first, block_width in zip(block_firsts, BLOCK_WIDTHS):
+            cols = slice(block_first, block_first + block_width)
+            turned = min(max(ROPE_COLS - block_first, 0), block_width)
+            for m in range(TOKEN_TILES):
+                acc = psum.tile([P, BANK], F32, tag="bank")
+                for g in range(PASSES):
+                    slot, plane = divmod(g, PLANES_PER_SLOT)
+                    nc.tensor.matmul_mx(
+                        out=acc[:, :block_width],
+                        lhsT=x_codes[:, PASSES * m + g, :].bitcast(FP8X4),
+                        lhsT_scale=x_scales[:, PASSES * m + g, :],
+                        rhs=w_codes[:, g, cols].bitcast(FP8X4),
+                        rhs_scale=w_scales[4 * plane : P, slot, cols],
+                        start=(g == 0),
+                        stop=(g == PASSES - 1),
+                    )
+
+                result = work.tile([P, BANK], F32)
+                if turned > 0:
+                    shape = [P, turned // HEAD, 2, HALF]
+                    halves = acc[:, :turned].rearrange("p (h s j) -> p h s j", s=2, j=HALF)
+                    from_high = work.tile([P, BANK], F32)
+                    nc.vector.tensor_tensor(
+                        out=result[:, :turned].rearrange("p (h s j) -> p h s j", s=2, j=HALF),
+                        in0=halves[:, :, 0:1, :].to_broadcast(shape),
+                        in1=for_low[:, m, :].rearrange("p (o s j) -> p o s j", o=1, s=2).to_broadcast(shape),
+                        op=MULT,
+                    )
+                    nc.vector.tensor_tensor(
+                        out=from_high[:, :turned].rearrange("p (h s j) -> p h s j", s=2, j=HALF),
+                        in0=halves[:, :, 1:2, :].to_broadcast(shape),
+                        in1=for_high[:, m, :].rearrange("p (o s j) -> p o s j", o=1, s=2).to_broadcast(shape),
+                        op=MULT,
+                    )
+                    nc.gpsimd.tensor_tensor(
+                        out=result[:, :turned], in0=result[:, :turned], in1=from_high[:, :turned], op=ADD
+                    )
+                if turned < block_width:
+                    copy = nc.vector.tensor_copy if turned > 0 else nc.scalar.copy
+                    copy(out=result[:, turned:block_width], in_=acc[:, turned:block_width])
+
+                for weight in weights:
+                    lo, hi = overlap(block_first, block_width, weight["first"], weight["width"])
+                    if lo < hi:
+                        nc.scalar.dma_start(
+                            out=weight["out"][m][:, lo - weight["first"] : hi - weight["first"]],
+                            in_=result[:, lo - block_first : hi - block_first],
+                        )

@@ -26,8 +26,11 @@ ROPE_COLS = Q_COLS + KV_COLS
 COLS = Q_COLS + 2 * KV_COLS
 BANK = 512
 
-BLOCK_WIDTHS = [BANK // 2] + [BANK] * 7
+BLOCK_WIDTHS = [BANK // 2] * 2 + [BANK] * 6 + [BANK // 2]
 assert sum(BLOCK_WIDTHS) == COLS
+Q_BLOCKS = 6
+assert sum(BLOCK_WIDTHS[:Q_BLOCKS]) == Q_COLS
+STORE_WIDTH = 1280
 
 WORDS_PER_PASS = K_PASS // 2
 UNITS_PER_BANK = 2
@@ -35,10 +38,6 @@ UNITS_PER_QUANTISE = 4
 PLANES_PER_SLOT = 4
 
 FLOPS = 2 * TOKENS * HIDDEN * COLS
-
-
-def overlap(first, width, other_first, other_width):
-    return max(first, other_first), min(first + width, other_first + other_width)
 
 
 def tile_gqattention_pa_kernel(
@@ -59,6 +58,8 @@ def tile_gqattention_pa_kernel(
         )
     block_firsts = [sum(BLOCK_WIDTHS[:b]) for b in range(len(BLOCK_WIDTHS))]
 
+    q_weight, k_weight, v_weight = weights
+
     with tc.manual_schedule(), tc.tile_pool(name="keep", bufs=1) as keep, tc.tile_pool(
         name="work", bufs=6
     ) as work, tc.psum_pool(name="psum", bufs=8) as psum:
@@ -73,6 +74,7 @@ def tile_gqattention_pa_kernel(
         sin_sb = keep.tile([P, TOKEN_TILES, HEAD], BF16)
         for_low = keep.tile([P, TOKEN_TILES, HEAD], F32)
         for_high = keep.tile([P, TOKEN_TILES, HEAD], F32)
+        result = keep.tile([P, TOKEN_TILES, COLS], F32)
 
         nc.vector.memset(w_scales[:].bitcast(I32), 0)
         make_identity(nc, identity[:])
@@ -92,30 +94,31 @@ def tile_gqattention_pa_kernel(
                         in_=weight["scales"][PLANES_PER_SLOT, rows, :],
                     )
 
+        def load_words(weight, first, width):
+            nc.sync.dma_start(
+                out=w_codes[:, :, weight["first"] + first : weight["first"] + first + width].bitcast(I32),
+                in_=weight["words"][:, :, first : first + width],
+            )
+
         x_tiles = x[0].rearrange("(p m) k -> m p k", m=TOKEN_TILES)
         for m in range(TOKEN_TILES):
             nc.sync.dma_start(out=x_sb[:, m, :], in_=x_tiles[m])
-        scales_loaded = set()
-        for block_first, block_width in zip(block_firsts, BLOCK_WIDTHS):
-            touched = []
-            for weight in weights:
-                lo, hi = overlap(block_first, block_width, weight["first"], weight["width"])
-                if lo < hi:
-                    touched.append((weight, lo, hi))
-            new = [weight for weight, lo, hi in touched if weight["first"] not in scales_loaded]
-            for weight in new:
-                load_scales(weight, 0)
-            for weight, lo, hi in touched:
-                nc.sync.dma_start(
-                    out=w_codes[:, :, lo:hi].bitcast(I32),
-                    in_=weight["words"][:, :, lo - weight["first"] : hi - weight["first"]],
-                )
-            for weight in new:
-                load_scales(weight, 1)
-                scales_loaded.add(weight["first"])
-            if block_first == 0:
-                nc.sync.dma_start(out=cos_sb[:], in_=cos_f.rearrange("(p m) d -> p m d", m=TOKEN_TILES))
-                nc.sync.dma_start(out=sin_sb[:], in_=sin_f.rearrange("(p m) d -> p m d", m=TOKEN_TILES))
+        load_scales(q_weight, 0)
+        load_words(q_weight, block_firsts[0], BLOCK_WIDTHS[0])
+        load_scales(q_weight, 1)
+        nc.sync.dma_start(out=cos_sb[:], in_=cos_f.rearrange("(p m) d -> p m d", m=TOKEN_TILES))
+        nc.sync.dma_start(out=sin_sb[:], in_=sin_f.rearrange("(p m) d -> p m d", m=TOKEN_TILES))
+        load_words(q_weight, block_firsts[1], BLOCK_WIDTHS[1])
+        load_words(q_weight, block_firsts[2], BLOCK_WIDTHS[2])
+        load_scales(k_weight, 0)
+        load_words(q_weight, block_firsts[3], BLOCK_WIDTHS[3])
+        load_scales(k_weight, 1)
+        load_words(q_weight, block_firsts[4], BLOCK_WIDTHS[4])
+        load_scales(v_weight, 0)
+        load_words(q_weight, block_firsts[5], BLOCK_WIDTHS[5])
+        load_scales(v_weight, 1)
+        load_words(k_weight, 0, KV_COLS)
+        load_words(v_weight, 0, KV_COLS)
 
         x_words = x_sb[:].bitcast(F32)
         grouped_words = grouped[:].bitcast(F32)
@@ -172,13 +175,13 @@ def tile_gqattention_pa_kernel(
                         stop=(g == PASSES - 1),
                     )
 
-                result = work.tile([P, BANK], F32)
+                done = result[:, m, cols]
                 if turned > 0:
                     shape = [P, turned // HEAD, 2, HALF]
                     halves = acc[:, :turned].rearrange("p (h s j) -> p h s j", s=2, j=HALF)
                     from_high = work.tile([P, BANK], F32)
                     nc.vector.tensor_tensor(
-                        out=result[:, :turned].rearrange("p (h s j) -> p h s j", s=2, j=HALF),
+                        out=done[:, :turned].rearrange("p (h s j) -> p h s j", s=2, j=HALF),
                         in0=halves[:, :, 0:1, :].to_broadcast(shape),
                         in1=for_low[:, m, :].rearrange("p (o s j) -> p o s j", o=1, s=2).to_broadcast(shape),
                         op=MULT,
@@ -190,16 +193,18 @@ def tile_gqattention_pa_kernel(
                         op=MULT,
                     )
                     nc.gpsimd.tensor_tensor(
-                        out=result[:, :turned], in0=result[:, :turned], in1=from_high[:, :turned], op=ADD
+                        out=done[:, :turned], in0=done[:, :turned], in1=from_high[:, :turned], op=ADD
                     )
                 if turned < block_width:
                     copy = nc.vector.tensor_copy if turned > 0 else nc.scalar.copy
-                    copy(out=result[:, turned:block_width], in_=acc[:, turned:block_width])
+                    copy(out=done[:, turned:], in_=acc[:, turned:block_width])
 
                 for weight in weights:
-                    lo, hi = overlap(block_first, block_width, weight["first"], weight["width"])
-                    if lo < hi:
-                        nc.scalar.dma_start(
-                            out=weight["out"][m][:, lo - weight["first"] : hi - weight["first"]],
-                            in_=result[:, lo - block_first : hi - block_first],
-                        )
+                    for piece in range(0, weight["width"], STORE_WIDTH):
+                        width = min(STORE_WIDTH, weight["width"] - piece)
+                        first = weight["first"] + piece
+                        if block_first < first + width <= block_first + block_width:
+                            nc.sync.dma_start(
+                                out=weight["out"][m][:, piece : piece + width],
+                                in_=result[:, m, first : first + width],
+                            )

@@ -30,7 +30,8 @@ BLOCK_WIDTHS = [BANK // 2] * 2 + [BANK] * 6 + [BANK // 2]
 assert sum(BLOCK_WIDTHS) == COLS
 Q_BLOCKS = 6
 assert sum(BLOCK_WIDTHS[:Q_BLOCKS]) == Q_COLS
-STORE_WIDTH = 1280
+EARLY_SCALE_COLS = sum(BLOCK_WIDTHS[:3])
+STORE_AFTER_BLOCKS = (3, 5, 7, 8)
 
 WORDS_PER_PASS = K_PASS // 2
 UNITS_PER_BANK = 2
@@ -79,19 +80,20 @@ def tile_gqattention_pa_kernel(
         nc.vector.memset(w_scales[:].bitcast(I32), 0)
         make_identity(nc, identity[:])
 
-        def load_scales(weight, slot):
-            cols = slice(weight["first"], weight["first"] + weight["width"])
+        def load_scales(weight, slot, first, width):
+            cols = slice(weight["first"] + first, weight["first"] + first + width)
+            int32_cols = slice(first // 4, (first + width) // 4)
             for quadrant in range(4):
                 rows = slice(4 * quadrant, 4 * quadrant + 4)
                 if slot == 0:
                     nc.sync.dma_start(
                         out=w_scales[32 * quadrant : 32 * quadrant + 16, 0, cols].bitcast(I32),
-                        in_=weight["scales"][0:PLANES_PER_SLOT, rows, :],
+                        in_=weight["scales"][0:PLANES_PER_SLOT, rows, int32_cols],
                     )
                 else:
                     nc.sync.dma_start(
                         out=w_scales[32 * quadrant : 32 * quadrant + 4, 1, cols].bitcast(I32),
-                        in_=weight["scales"][PLANES_PER_SLOT, rows, :],
+                        in_=weight["scales"][PLANES_PER_SLOT, rows, int32_cols],
                     )
 
         def load_words(weight, first, width):
@@ -103,22 +105,25 @@ def tile_gqattention_pa_kernel(
         x_tiles = x[0].rearrange("(p m) k -> m p k", m=TOKEN_TILES)
         for m in range(TOKEN_TILES):
             nc.sync.dma_start(out=x_sb[:, m, :], in_=x_tiles[m])
-        load_scales(q_weight, 0)
+        late_scale_cols = Q_COLS - EARLY_SCALE_COLS
+        load_scales(q_weight, 0, 0, EARLY_SCALE_COLS)
         load_words(q_weight, block_firsts[0], BLOCK_WIDTHS[0])
-        load_scales(q_weight, 1)
+        load_scales(q_weight, 1, 0, EARLY_SCALE_COLS)
         nc.sync.dma_start(out=cos_sb[:], in_=cos_f.rearrange("(p m) d -> p m d", m=TOKEN_TILES))
         nc.sync.dma_start(out=sin_sb[:], in_=sin_f.rearrange("(p m) d -> p m d", m=TOKEN_TILES))
         load_words(q_weight, block_firsts[1], BLOCK_WIDTHS[1])
         load_words(q_weight, block_firsts[2], BLOCK_WIDTHS[2])
-        load_scales(k_weight, 0)
+        load_scales(q_weight, 0, EARLY_SCALE_COLS, late_scale_cols)
         load_words(q_weight, block_firsts[3], BLOCK_WIDTHS[3])
-        load_scales(k_weight, 1)
+        load_scales(q_weight, 1, EARLY_SCALE_COLS, late_scale_cols)
         load_words(q_weight, block_firsts[4], BLOCK_WIDTHS[4])
-        load_scales(v_weight, 0)
+        load_scales(k_weight, 0, 0, KV_COLS)
         load_words(q_weight, block_firsts[5], BLOCK_WIDTHS[5])
-        load_scales(v_weight, 1)
+        load_scales(k_weight, 1, 0, KV_COLS)
         load_words(k_weight, 0, KV_COLS)
+        load_scales(v_weight, 0, 0, KV_COLS)
         load_words(v_weight, 0, KV_COLS)
+        load_scales(v_weight, 1, 0, KV_COLS)
 
         x_words = x_sb[:].bitcast(F32)
         grouped_words = grouped[:].bitcast(F32)
@@ -158,8 +163,10 @@ def tile_gqattention_pa_kernel(
         nc.scalar.mul(out=for_high[:, :, :HALF], in_=sin_sb[:, :, :HALF], mul=-1.0)
         nc.scalar.copy(out=for_high[:, :, HALF:], in_=cos_sb[:, :, HALF:])
 
-        for block_first, block_width in zip(block_firsts, BLOCK_WIDTHS):
-            cols = slice(block_first, block_first + block_width)
+        stored = 0
+        for b, (block_first, block_width) in enumerate(zip(block_firsts, BLOCK_WIDTHS)):
+            block_end = block_first + block_width
+            cols = slice(block_first, block_end)
             turned = min(max(ROPE_COLS - block_first, 0), block_width)
             for m in range(TOKEN_TILES):
                 acc = psum.tile([P, BANK], F32, tag="bank")
@@ -199,12 +206,14 @@ def tile_gqattention_pa_kernel(
                     copy = nc.vector.tensor_copy if turned > 0 else nc.scalar.copy
                     copy(out=done[:, turned:], in_=acc[:, turned:block_width])
 
-                for weight in weights:
-                    for piece in range(0, weight["width"], STORE_WIDTH):
-                        width = min(STORE_WIDTH, weight["width"] - piece)
-                        first = weight["first"] + piece
-                        if block_first < first + width <= block_first + block_width:
+                if b in STORE_AFTER_BLOCKS:
+                    for weight in weights:
+                        first = max(stored, weight["first"])
+                        end = min(block_end, weight["first"] + weight["width"])
+                        if first < end:
                             nc.sync.dma_start(
-                                out=weight["out"][m][:, piece : piece + width],
-                                in_=result[:, m, first : first + width],
+                                out=weight["out"][m][:, first - weight["first"] : end - weight["first"]],
+                                in_=result[:, m, first:end],
                             )
+            if b in STORE_AFTER_BLOCKS:
+                stored = block_end

@@ -38,6 +38,9 @@ UNITS_PER_BANK = 2
 UNITS_PER_QUANTISE = 4
 PLANES_PER_SLOT = 4
 
+WARM_UP = 9
+BETWEEN_RUNS = 2
+
 FLOPS = 2 * TOKENS * HIDDEN * COLS
 
 
@@ -76,6 +79,14 @@ def tile_gqattention_pa_kernel(
         for_low = keep.tile([P, TOKEN_TILES, HEAD], F32)
         for_high = keep.tile([P, TOKEN_TILES, HEAD], F32)
         result = keep.tile([P, TOKEN_TILES, COLS], F32)
+
+        zeros = keep.tile([P, BANK], BF16)
+        nc.vector.memset(zeros[:], 0.0)
+
+        def keep_clock(count):
+            unread = psum.tile([P, BANK], F32, tag="bank")
+            for i in range(count):
+                nc.tensor.matmul(unread[:], lhsT=zeros[:, :P], rhs=zeros[:], start=True, stop=True)
 
         nc.vector.memset(w_scales[:].bitcast(I32), 0)
         make_identity(nc, identity[:])
@@ -151,7 +162,10 @@ def tile_gqattention_pa_kernel(
                 in_=grouped[:, units, :, :].rearrange("p a t j -> p (a t j)"),
             )
 
+        keep_clock(WARM_UP)
         for first_unit in range(0, UNITS, UNITS_PER_QUANTISE):
+            if first_unit > 0:
+                keep_clock(BETWEEN_RUNS)
             transpose_units(first_unit, nc.vector.tensor_copy)
             transpose_units(first_unit + UNITS_PER_BANK, nc.scalar.copy)
             if first_unit > 0:

@@ -125,16 +125,16 @@ def tile_gqattention_pa_kernel(
         load_words(q_weight, block_firsts[1], BLOCK_WIDTHS[1])
         load_words(q_weight, block_firsts[2], BLOCK_WIDTHS[2])
         load_scales(q_weight, 0, EARLY_SCALE_COLS, late_scale_cols)
-        load_words(q_weight, block_firsts[3], BLOCK_WIDTHS[3])
         load_scales(q_weight, 1, EARLY_SCALE_COLS, late_scale_cols)
+        load_words(q_weight, block_firsts[3], BLOCK_WIDTHS[3])
         load_words(q_weight, block_firsts[4], BLOCK_WIDTHS[4])
-        load_scales(k_weight, 0, 0, KV_COLS)
         load_words(q_weight, block_firsts[5], BLOCK_WIDTHS[5])
+        load_scales(k_weight, 0, 0, KV_COLS)
         load_scales(k_weight, 1, 0, KV_COLS)
-        load_words(k_weight, 0, KV_COLS)
         load_scales(v_weight, 0, 0, KV_COLS)
-        load_words(v_weight, 0, KV_COLS)
         load_scales(v_weight, 1, 0, KV_COLS)
+        load_words(k_weight, 0, KV_COLS)
+        load_words(v_weight, 0, KV_COLS)
 
         x_words = x_sb[:].bitcast(F32)
         grouped_words = grouped[:].bitcast(F32)

@@ -217,8 +217,7 @@ def tile_gqattention_pa_kernel(
                         out=done[:, :turned], in0=done[:, :turned], in1=from_high[:, :turned], op=ADD
                     )
                 if turned < block_width:
-                    copy = nc.vector.tensor_copy if turned > 0 else nc.scalar.copy
-                    copy(out=done[:, turned:], in_=acc[:, turned:block_width])
+                    nc.scalar.copy(out=done[:, turned:], in_=acc[:, turned:block_width])
 
                 if b in STORE_AFTER_BLOCKS:
                     for weight in weights:

@@ -26,12 +26,12 @@ ROPE_COLS = Q_COLS + KV_COLS
 COLS = Q_COLS + 2 * KV_COLS
 BANK = 512
 
-BLOCK_WIDTHS = [BANK // 2] * 2 + [BANK] * 6 + [BANK // 2]
+BLOCK_WIDTHS = [BANK] * 7 + [BANK // 2]
 assert sum(BLOCK_WIDTHS) == COLS
-Q_BLOCKS = 6
+Q_BLOCKS = 5
 assert sum(BLOCK_WIDTHS[:Q_BLOCKS]) == Q_COLS
 EARLY_SCALE_COLS = sum(BLOCK_WIDTHS[:3])
-STORE_AFTER_BLOCKS = (3, 5, 7, 8)
+STORE_AFTER_BLOCKS = (2, 4, 6, 7)
 
 WORDS_PER_PASS = K_PASS // 2
 UNITS_PER_BANK = 2
@@ -39,7 +39,6 @@ UNITS_PER_QUANTISE = 4
 PLANES_PER_SLOT = 4
 
 WARM_UP = 9
-BETWEEN_RUNS = 2
 
 FLOPS = 2 * TOKENS * HIDDEN * COLS
 
@@ -118,7 +117,10 @@ def tile_gqattention_pa_kernel(
             nc.sync.dma_start(out=x_sb[:, m, :], in_=x_tiles[m])
         late_scale_cols = Q_COLS - EARLY_SCALE_COLS
         load_scales(q_weight, 0, 0, EARLY_SCALE_COLS)
-        load_words(q_weight, block_firsts[0], BLOCK_WIDTHS[0])
+        for g in range(PASSES):
+            nc.sync.dma_start(
+                out=w_codes[:, g, : BLOCK_WIDTHS[0]].bitcast(I32), in_=q_weight["words"][:, g, : BLOCK_WIDTHS[0]]
+            )
         load_scales(q_weight, 1, 0, EARLY_SCALE_COLS)
         nc.sync.dma_start(out=cos_sb[:], in_=cos_f.rearrange("(p m) d -> p m d", m=TOKEN_TILES))
         nc.sync.dma_start(out=sin_sb[:], in_=sin_f.rearrange("(p m) d -> p m d", m=TOKEN_TILES))
@@ -128,7 +130,6 @@ def tile_gqattention_pa_kernel(
         load_scales(q_weight, 1, EARLY_SCALE_COLS, late_scale_cols)
         load_words(q_weight, block_firsts[3], BLOCK_WIDTHS[3])
         load_words(q_weight, block_firsts[4], BLOCK_WIDTHS[4])
-        load_words(q_weight, block_firsts[5], BLOCK_WIDTHS[5])
         load_scales(k_weight, 0, 0, KV_COLS)
         load_scales(k_weight, 1, 0, KV_COLS)
         load_scales(v_weight, 0, 0, KV_COLS)
@@ -164,8 +165,6 @@ def tile_gqattention_pa_kernel(
 
         keep_clock(WARM_UP)
         for first_unit in range(0, UNITS, UNITS_PER_QUANTISE):
-            if first_unit > 0:
-                keep_clock(BETWEEN_RUNS)
             transpose_units(first_unit, nc.vector.tensor_copy)
             transpose_units(first_unit + UNITS_PER_BANK, nc.scalar.copy)
             if first_unit > 0:
@@ -182,19 +181,35 @@ def tile_gqattention_pa_kernel(
             block_end = block_first + block_width
             cols = slice(block_first, block_end)
             turned = min(max(ROPE_COLS - block_first, 0), block_width)
-            for m in range(TOKEN_TILES):
-                acc = psum.tile([P, BANK], F32, tag="bank")
+
+            def one_pass(acc, m, g):
+                slot, plane = divmod(g, PLANES_PER_SLOT)
+                nc.tensor.matmul_mx(
+                    out=acc[:, :block_width],
+                    lhsT=x_codes[:, PASSES * m + g, :].bitcast(FP8X4),
+                    lhsT_scale=x_scales[:, PASSES * m + g, :],
+                    rhs=w_codes[:, g, cols].bitcast(FP8X4),
+                    rhs_scale=w_scales[4 * plane : P, slot, cols],
+                    start=(g == 0),
+                    stop=(g == PASSES - 1),
+                )
+
+            open_banks = []
+            if b == 0:
+                for m in range(TOKEN_TILES):
+                    first_acc = psum.tile([P, BANK], F32, tag="bank", name="first_acc%d" % m)
+                    open_banks.append(first_acc)
                 for g in range(PASSES):
-                    slot, plane = divmod(g, PLANES_PER_SLOT)
-                    nc.tensor.matmul_mx(
-                        out=acc[:, :block_width],
-                        lhsT=x_codes[:, PASSES * m + g, :].bitcast(FP8X4),
-                        lhsT_scale=x_scales[:, PASSES * m + g, :],
-                        rhs=w_codes[:, g, cols].bitcast(FP8X4),
-                        rhs_scale=w_scales[4 * plane : P, slot, cols],
-                        start=(g == 0),
-                        stop=(g == PASSES - 1),
-                    )
+                    for m in range(TOKEN_TILES):
+                        one_pass(open_banks[m], m, g)
+
+            for m in range(TOKEN_TILES):
+                if b == 0:
+                    acc = open_banks[m]
+                else:
+                    acc = psum.tile([P, BANK], F32, tag="bank")
+                    for g in range(PASSES):
+                        one_pass(acc, m, g)
 
                 done = result[:, m, cols]
                 if turned > 0:

@@ -57,6 +57,7 @@ def tile_gqattention_pa_kernel(
                 "words": words.rearrange("g p n t -> p g (n t)").bitcast(I32),
                 "scales": scales.bitcast(I32),
                 "out": out[0].rearrange("(p m) h d -> m p (h d)", m=TOKEN_TILES),
+                "out_all_tiles": out[0].rearrange("(p m) h d -> p m (h d)", m=TOKEN_TILES),
             }
         )
     block_firsts = [sum(BLOCK_WIDTHS[:b]) for b in range(len(BLOCK_WIDTHS))]
@@ -234,7 +235,7 @@ def tile_gqattention_pa_kernel(
                 if turned < block_width:
                     nc.scalar.copy(out=done[:, turned:], in_=acc[:, turned:block_width])
 
-                if b in STORE_AFTER_BLOCKS:
+                if b in STORE_AFTER_BLOCKS and b >= Q_BLOCKS:
                     for weight in weights:
                         first = max(stored, weight["first"])
                         end = min(block_end, weight["first"] + weight["width"])
@@ -243,5 +244,7 @@ def tile_gqattention_pa_kernel(
                                 out=weight["out"][m][:, first - weight["first"] : end - weight["first"]],
                                 in_=result[:, m, first:end],
                             )
+            if b in STORE_AFTER_BLOCKS and b < Q_BLOCKS:
+                nc.sync.dma_start(out=q_weight["out_all_tiles"][:, :, stored:block_end], in_=result[:, :, stored:block_end])
             if b in STORE_AFTER_BLOCKS:
                 stored = block_end

@@ -38,7 +38,6 @@ UNITS_PER_BANK = 2
 UNITS_PER_QUANTISE = 4
 PLANES_PER_SLOT = 4
 
-WARM_UP = 9
 
 FLOPS = 2 * TOKENS * HIDDEN * COLS
 
@@ -79,14 +78,6 @@ def tile_gqattention_pa_kernel(
         for_low = keep.tile([P, TOKEN_TILES, HEAD], F32)
         for_high = keep.tile([P, TOKEN_TILES, HEAD], F32)
         result = keep.tile([P, TOKEN_TILES, COLS], F32)
-
-        zeros = keep.tile([P, BANK], BF16)
-        nc.vector.memset(zeros[:], 0.0)
-
-        def keep_clock(count):
-            unread = psum.tile([P, BANK], F32, tag="bank")
-            for i in range(count):
-                nc.tensor.matmul(unread[:], lhsT=zeros[:, :P], rhs=zeros[:], start=True, stop=True)
 
         nc.vector.memset(w_scales[:].bitcast(I32), 0)
         make_identity(nc, identity[:])
@@ -164,7 +155,6 @@ def tile_gqattention_pa_kernel(
                 in_=grouped[:, units, :, :].rearrange("p a t j -> p (a t j)"),
             )
 
-        keep_clock(WARM_UP)
         for first_unit in range(0, UNITS, UNITS_PER_QUANTISE):
             transpose_units(first_unit, nc.vector.tensor_copy)
             transpose_units(first_unit + UNITS_PER_BANK, nc.scalar.copy)

@@ -30,7 +30,8 @@ BLOCK_WIDTHS = [BANK] * 7 + [BANK // 2]
 assert sum(BLOCK_WIDTHS) == COLS
 Q_BLOCKS = 5
 assert sum(BLOCK_WIDTHS[:Q_BLOCKS]) == Q_COLS
-EARLY_SCALE_COLS = sum(BLOCK_WIDTHS[:3])
+EARLY_WORD_COLS = sum(BLOCK_WIDTHS[:2])
+EARLY_SCALE_COLS = EARLY_WORD_COLS
 STORE_AFTER_BLOCKS = (2, 4, 6, 7)
 
 WORDS_PER_PASS = K_PASS // 2
@@ -109,17 +110,23 @@ def tile_gqattention_pa_kernel(
             nc.sync.dma_start(out=x_sb[:, m, :], in_=x_tiles[m])
         late_scale_cols = Q_COLS - EARLY_SCALE_COLS
         load_scales(q_weight, 0, 0, EARLY_SCALE_COLS)
-        for g in range(PASSES):
+
+        def load_early_words(g):
             nc.sync.dma_start(
-                out=w_codes[:, g, : BLOCK_WIDTHS[0]].bitcast(I32), in_=q_weight["words"][:, g, : BLOCK_WIDTHS[0]]
+                out=w_codes[:, g, :EARLY_WORD_COLS].bitcast(I32), in_=q_weight["words"][:, g, :EARLY_WORD_COLS]
             )
+
+        load_early_words(0)
+        load_early_words(1)
+        load_early_words(2)
         load_scales(q_weight, 1, 0, EARLY_SCALE_COLS)
+        load_early_words(3)
         nc.sync.dma_start(out=cos_sb[:], in_=cos_f.rearrange("(p m) d -> p m d", m=TOKEN_TILES))
         nc.sync.dma_start(out=sin_sb[:], in_=sin_f.rearrange("(p m) d -> p m d", m=TOKEN_TILES))
-        load_words(q_weight, block_firsts[1], BLOCK_WIDTHS[1])
-        load_words(q_weight, block_firsts[2], BLOCK_WIDTHS[2])
+        load_early_words(4)
         load_scales(q_weight, 0, EARLY_SCALE_COLS, late_scale_cols)
         load_scales(q_weight, 1, EARLY_SCALE_COLS, late_scale_cols)
+        load_words(q_weight, block_firsts[2], BLOCK_WIDTHS[2])
         load_words(q_weight, block_firsts[3], BLOCK_WIDTHS[3])
         load_words(q_weight, block_firsts[4], BLOCK_WIDTHS[4])
         load_scales(k_weight, 0, 0, KV_COLS)

@@ -127,8 +127,7 @@ def tile_gqattention_pa_kernel(
         load_scales(q_weight, 0, EARLY_SCALE_COLS, late_scale_cols)
         load_scales(q_weight, 1, EARLY_SCALE_COLS, late_scale_cols)
         load_words(q_weight, block_firsts[2], BLOCK_WIDTHS[2])
-        load_words(q_weight, block_firsts[3], BLOCK_WIDTHS[3])
-        load_words(q_weight, block_firsts[4], BLOCK_WIDTHS[4])
+        load_words(q_weight, block_firsts[3], BLOCK_WIDTHS[3] + BLOCK_WIDTHS[4])
         load_scales(k_weight, 0, 0, KV_COLS)
         load_scales(k_weight, 1, 0, KV_COLS)
         load_scales(v_weight, 0, 0, KV_COLS)
@@ -233,7 +232,7 @@ def tile_gqattention_pa_kernel(
                     nc.scalar.copy(out=done[:, turned:], in_=acc[:, turned:block_width])
 
                 if b in STORE_AFTER_BLOCKS and b >= Q_BLOCKS:
-                    for weight in weights:
+                    for weight in reversed(weights):
                         first = max(stored, weight["first"])
                         end = min(block_end, weight["first"] + weight["width"])
                         if first < end:

import concourse.mybir as mybir
from concourse.masks import make_identity

F32 = mybir.dt.float32
BF16 = mybir.dt.bfloat16
I32 = mybir.dt.int32
U32 = mybir.dt.uint32
U8 = mybir.dt.uint8
FP8X4 = mybir.dt.float8_e4m3fn_x4
MULT = mybir.AluOpType.mult
ADD = mybir.AluOpType.add

P = 128
PACK = 4
K_PASS = P * PACK
TOKENS = 512
HIDDEN = 2560
PASSES = HIDDEN // K_PASS
TOKEN_TILES = TOKENS // P
UNITS = TOKEN_TILES * PASSES
HEAD = 128
HALF = HEAD // 2
Q_COLS = 20 * HEAD
KV_COLS = 5 * HEAD
ROPE_COLS = Q_COLS + KV_COLS
COLS = Q_COLS + 2 * KV_COLS
BANK = 512

BLOCK_WIDTHS = [BANK] * 7 + [BANK // 2]
assert sum(BLOCK_WIDTHS) == COLS
Q_BLOCKS = 5
assert sum(BLOCK_WIDTHS[:Q_BLOCKS]) == Q_COLS
EARLY_WORD_COLS = sum(BLOCK_WIDTHS[:2])
EARLY_SCALE_COLS = EARLY_WORD_COLS
STORE_AFTER_BLOCKS = (2, 4, 6, 7)

WORDS_PER_PASS = K_PASS // 2
UNITS_PER_BANK = 2
UNITS_PER_QUANTISE = 4
PLANES_PER_SLOT = 4


FLOPS = 2 * TOKENS * HIDDEN * COLS


def tile_gqattention_pa_kernel(
    tc, x, cos_f, sin_f, Wq_words, Wq_scales, Wk_words, Wk_scales, Wv_words, Wv_scales, out_0, out_1, out_2
):
    nc = tc.nc

    weights = []
    for words, scales, out in ((Wq_words, Wq_scales, out_0), (Wk_words, Wk_scales, out_1), (Wv_words, Wv_scales, out_2)):
        weights.append(
            {
                "first": sum(w["width"] for w in weights),
                "width": words.shape[2],
                "words": words.rearrange("g p n t -> p g (n t)").bitcast(I32),
                "scales": scales.bitcast(I32),
                "out": out[0].rearrange("(p m) h d -> m p (h d)", m=TOKEN_TILES),
                "out_all_tiles": out[0].rearrange("(p m) h d -> p m (h d)", m=TOKEN_TILES),
            }
        )
    block_firsts = [sum(BLOCK_WIDTHS[:b]) for b in range(len(BLOCK_WIDTHS))]

    q_weight, k_weight, v_weight = weights

    with tc.manual_schedule(), tc.tile_pool(name="keep", bufs=1) as keep, tc.tile_pool(
        name="work", bufs=6
    ) as work, tc.psum_pool(name="psum", bufs=8) as psum:
        x_sb = keep.tile([P, TOKEN_TILES, HIDDEN], BF16)
        grouped = keep.tile([P, UNITS, P, PACK], BF16, align_bytes=64)
        x_codes = keep.tile([P, UNITS, P], U32, align_bytes=64)
        x_scales = keep.tile([P, UNITS, P], U8, align_bytes=64)
        w_codes = keep.tile([P, PASSES, COLS], U32, align_bytes=64)
        w_scales = keep.tile([P, 2, COLS], U8, align_bytes=64)
        identity = keep.tile([P, P], F32)
        cos_sb = keep.tile([P, TOKEN_TILES, HEAD], BF16)
        sin_sb = keep.tile([P, TOKEN_TILES, HEAD], BF16)
        for_low = keep.tile([P, TOKEN_TILES, HEAD], F32)
        for_high = keep.tile([P, TOKEN_TILES, HEAD], F32)
        result = keep.tile([P, TOKEN_TILES, COLS], F32)

        nc.vector.memset(w_scales[:].bitcast(I32), 0)
        make_identity(nc, identity[:])

        def load_scales(weight, slot, first, width):
            cols = slice(weight["first"] + first, weight["first"] + first + width)
            int32_cols = slice(first // 4, (first + width) // 4)
            for quadrant in range(4):
                rows = slice(4 * quadrant, 4 * quadrant + 4)
                if slot == 0:
                    nc.sync.dma_start(
                        out=w_scales[32 * quadrant : 32 * quadrant + 16, 0, cols].bitcast(I32),
                        in_=weight["scales"][0:PLANES_PER_SLOT, rows, int32_cols],
                    )
                else:
                    nc.sync.dma_start(
                        out=w_scales[32 * quadrant : 32 * quadrant + 4, 1, cols].bitcast(I32),
                        in_=weight["scales"][PLANES_PER_SLOT, rows, int32_cols],
                    )

        def load_words(weight, first, width):
            nc.sync.dma_start(
                out=w_codes[:, :, weight["first"] + first : weight["first"] + first + width].bitcast(I32),
                in_=weight["words"][:, :, first : first + width],
            )

        x_tiles = x[0].rearrange("(p m) k -> m p k", m=TOKEN_TILES)
        for m in range(TOKEN_TILES):
            nc.sync.dma_start(out=x_sb[:, m, :], in_=x_tiles[m])
        late_scale_cols = Q_COLS - EARLY_SCALE_COLS
        load_scales(q_weight, 0, 0, EARLY_SCALE_COLS)

        def load_early_words(g):
            nc.sync.dma_start(
                out=w_codes[:, g, :EARLY_WORD_COLS].bitcast(I32), in_=q_weight["words"][:, g, :EARLY_WORD_COLS]
            )

        load_early_words(0)
        load_early_words(1)
        load_early_words(2)
        load_scales(q_weight, 1, 0, EARLY_SCALE_COLS)
        load_early_words(3)
        nc.sync.dma_start(out=cos_sb[:], in_=cos_f.rearrange("(p m) d -> p m d", m=TOKEN_TILES))
        nc.sync.dma_start(out=sin_sb[:], in_=sin_f.rearrange("(p m) d -> p m d", m=TOKEN_TILES))
        load_early_words(4)
        load_scales(q_weight, 0, EARLY_SCALE_COLS, late_scale_cols)
        load_scales(q_weight, 1, EARLY_SCALE_COLS, late_scale_cols)
        load_words(q_weight, block_firsts[2], BLOCK_WIDTHS[2])
        load_words(q_weight, block_firsts[3], BLOCK_WIDTHS[3] + BLOCK_WIDTHS[4])
        load_scales(k_weight, 0, 0, KV_COLS)
        load_scales(k_weight, 1, 0, KV_COLS)
        load_scales(v_weight, 0, 0, KV_COLS)
        load_scales(v_weight, 1, 0, KV_COLS)
        load_words(k_weight, 0, KV_COLS)
        load_words(v_weight, 0, KV_COLS)

        x_words = x_sb[:].bitcast(F32)
        grouped_words = grouped[:].bitcast(F32)

        def transpose_units(first_unit, copy):
            bank = psum.tile([P, UNITS_PER_BANK, 2, P], F32, tag="bank")
            for a in range(UNITS_PER_BANK):
                m, g = divmod(first_unit + a, PASSES)
                for u in range(2):
                    nc.tensor.transpose(
                        bank[:, a, u, :],
                        x_words[:, m, WORDS_PER_PASS * g + u : WORDS_PER_PASS * (g + 1) : 2],
                        identity[:],
                    )
            copy(
                out=grouped_words[:, first_unit : first_unit + UNITS_PER_BANK, :, :],
                in_=bank[:].rearrange("p a u t -> p a t u"),
            )

        def quantise_units(first_unit):
            units = slice(first_unit, first_unit + UNITS_PER_QUANTISE)
            nc.vector.quantize_mx(
                out=x_codes[:, units, :].rearrange("p a t -> p (a t)").bitcast(FP8X4),
                scales=x_scales[:, units, :].rearrange("p a t -> p (a t)"),
                in_=grouped[:, units, :, :].rearrange("p a t j -> p (a t j)"),
            )

        for first_unit in range(0, UNITS, UNITS_PER_QUANTISE):
            transpose_units(first_unit, nc.vector.tensor_copy)
            transpose_units(first_unit + UNITS_PER_BANK, nc.scalar.copy)
            if first_unit > 0:
                quantise_units(first_unit - UNITS_PER_QUANTISE)
        quantise_units(UNITS - UNITS_PER_QUANTISE)

        nc.scalar.copy(out=for_low[:, :, :HALF], in_=cos_sb[:, :, :HALF])
        nc.scalar.copy(out=for_low[:, :, HALF:], in_=sin_sb[:, :, HALF:])
        nc.scalar.mul(out=for_high[:, :, :HALF], in_=sin_sb[:, :, :HALF], mul=-1.0)
        nc.scalar.copy(out=for_high[:, :, HALF:], in_=cos_sb[:, :, HALF:])

        stored = 0
        for b, (block_first, block_width) in enumerate(zip(block_firsts, BLOCK_WIDTHS)):
            block_end = block_first + block_width
            cols = slice(block_first, block_end)
            turned = min(max(ROPE_COLS - block_first, 0), block_width)

            def one_pass(acc, m, g):
                slot, plane = divmod(g, PLANES_PER_SLOT)
                nc.tensor.matmul_mx(
                    out=acc[:, :block_width],
                    lhsT=x_codes[:, PASSES * m + g, :].bitcast(FP8X4),
                    lhsT_scale=x_scales[:, PASSES * m + g, :],
                    rhs=w_codes[:, g, cols].bitcast(FP8X4),
                    rhs_scale=w_scales[4 * plane : P, slot, cols],
                    start=(g == 0),
                    stop=(g == PASSES - 1),
                )

            open_banks = []
            if b == 0:
                for m in range(TOKEN_TILES):
                    first_acc = psum.tile([P, BANK], F32, tag="bank", name="first_acc%d" % m)
                    open_banks.append(first_acc)
                for g in range(PASSES):
                    for m in range(TOKEN_TILES):
                        one_pass(open_banks[m], m, g)

            for m in range(TOKEN_TILES):
                if b == 0:
                    acc = open_banks[m]
                else:
                    acc = psum.tile([P, BANK], F32, tag="bank")
                    for g in range(PASSES):
                        one_pass(acc, m, g)

                done = result[:, m, cols]
                if turned > 0:
                    shape = [P, turned // HEAD, 2, HALF]
                    halves = acc[:, :turned].rearrange("p (h s j) -> p h s j", s=2, j=HALF)
                    from_high = work.tile([P, BANK], F32)
                    nc.vector.tensor_tensor(
                        out=done[:, :turned].rearrange("p (h s j) -> p h s j", s=2, j=HALF),
                        in0=halves[:, :, 0:1, :].to_broadcast(shape),
                        in1=for_low[:, m, :].rearrange("p (o s j) -> p o s j", o=1, s=2).to_broadcast(shape),
                        op=MULT,
                    )
                    nc.vector.tensor_tensor(
                        out=from_high[:, :turned].rearrange("p (h s j) -> p h s j", s=2, j=HALF),
                        in0=halves[:, :, 1:2, :].to_broadcast(shape),
                        in1=for_high[:, m, :].rearrange("p (o s j) -> p o s j", o=1, s=2).to_broadcast(shape),
                        op=MULT,
                    )
                    nc.gpsimd.tensor_tensor(
                        out=done[:, :turned], in0=done[:, :turned], in1=from_high[:, :turned], op=ADD
                    )
                if turned < block_width:
                    nc.scalar.copy(out=done[:, turned:], in_=acc[:, turned:block_width])

                if b in STORE_AFTER_BLOCKS and b >= Q_BLOCKS:
                    for weight in reversed(weights):
                        first = max(stored, weight["first"])
                        end = min(block_end, weight["first"] + weight["width"])
                        if first < end:
                            nc.sync.dma_start(
                                out=weight["out"][m][:, first - weight["first"] : end - weight["first"]],
                                in_=result[:, m, first:end],
                            )
            if b in STORE_AFTER_BLOCKS and b < Q_BLOCKS:
                nc.sync.dma_start(out=q_weight["out_all_tiles"][:, :, stored:block_end], in_=result[:, :, stored:block_end])
            if b in STORE_AFTER_BLOCKS:
                stored = block_end
